import numpy as np
import ml_dtypes


def mxq(x, axis, fmt="e4m3"):
    dtype, down = {"e4m3": (ml_dtypes.float8_e4m3fn, 7), "e5m2": (ml_dtypes.float8_e5m2, 14)}[fmt]
    v = np.moveaxis(np.asarray(x, np.float32).astype(ml_dtypes.bfloat16).astype(np.float64), axis, -1)
    blocks = v.reshape(v.shape[:-1] + (-1, 32))
    amax = np.abs(blocks).max(-1, keepdims=True)
    byte = np.maximum(np.where(amax > 0, np.frexp(amax)[1] - 1 + 127, 0) - down, 1)
    scale = np.exp2(byte - 127.0)
    codes = (blocks / scale).astype(np.float32).astype(dtype).astype(np.float64)
    return np.moveaxis((codes * scale).reshape(v.shape), -1, axis)


WIDE = False


def mx_kscale(k):
    if not WIDE:
        return np.ones(k)
    levels = np.array([10, -10, 5, -5, 0])
    a = np.random.permutation(np.resize(levels, k // 512 * 4)).reshape(k // 512, 4)
    idx = np.arange(k)
    return np.exp2(a[idx // 512, idx % 128 // 32])


BF16 = ml_dtypes.bfloat16


def bf(x):
    return np.asarray(x, np.float32).astype(BF16)


def f64(x):
    return np.asarray(x).astype(np.float64)


B, L, D, C, H, DFF, TE = 32, 32, 512, 512, 8, 2048, 1000
EPS = 1e-5
HS, NT = 0.5, 13


def erf(z):
    z2 = z * z
    s = np.zeros_like(z2)
    w = np.empty_like(z2)
    for n in range(NT):
        t2 = ((n + 0.5) * HS) ** 2
        np.add(z2, t2, out=w)
        np.divide(np.exp(-t2), w, out=w)
        s += w
    return np.tanh(np.pi / HS * z) - 2.0 * HS / np.pi * z * np.exp(-z2) * s


def gelu(v):
    return 0.5 * v * (1.0 + erf(v / np.sqrt(2.0)))


def layer_norm(v, g, b):
    d = v - v.mean(-1, keepdims=True)
    var = (d * d).mean(-1, keepdims=True)
    return d / np.sqrt(var + EPS) * g + b


def setup_inputs():
    r = np.random.standard_normal
    s = mx_kscale(D)
    s2 = np.concatenate([s, s])
    return {"x_attn": bf(r((B, L, D)) * s),
            "cw1": bf(r((2 * D, C)) * 0.7 / np.sqrt(D) / s2[:, None]),
            "cb1": bf(r(C) * 0.3),
            "cw2": bf(r((C, D)) / np.sqrt(C)),
            "cb2": bf(r(D) * 0.3),
            "cln_g": bf(1.0 + 0.2 * r(D)),
            "cln_b": bf(r(D) * 0.2)}


def reference(x_attn, cw1, cb1, cw2, cb2, cln_g, cln_b):
    xq = mxq(f64(x_attn), 2, "e4m3")
    w1 = f64(cw1)
    a = xq @ mxq(w1[:D], 0, "e4m3")
    e = xq @ mxq(w1[D:], 0, "e4m3")
    i, j = np.tril_indices(L)
    h2 = gelu(a[:, i] + e[:, j] + f64(cb1))
    y = (mxq(h2, 2, "e4m3") @ mxq(f64(cw2), 0, "e4m3")) + f64(cb2)
    rel = layer_norm(y, f64(cln_g), f64(cln_b))
    return np.stack([rel[:, i == n].sum(axis=1) for n in range(L)], axis=1) / L

@@ -1,0 +1,269 @@
+from contextlib import ExitStack
+
+import concourse.mybir as mybir
+from concourse.masks import make_identity
+
+F32 = mybir.dt.float32
+BF16 = mybir.dt.bfloat16
+I32 = mybir.dt.int32
+U32 = mybir.dt.uint32
+U8 = mybir.dt.uint8
+FP8X4 = mybir.dt.float8_e4m3fn_x4
+ALU = mybir.AluOpType
+ACT = mybir.ActivationFunctionType
+
+P = 128
+PACK = 4
+BATCH, LENGTH, WIDTH = 32, 32, 512
+EPS = 1e-5
+CHUNKS = WIDTH // P
+GROUP_BATCH = 8
+GROUPS = BATCH // GROUP_BATCH
+GROUP_ROWS = GROUP_BATCH * LENGTH
+DIAGONAL = -1
+
+FLOPS = 2 * BATCH * LENGTH * WIDTH * 2 * WIDTH + 2 * BATCH * (LENGTH * (LENGTH + 1) // 2) * WIDTH * WIDTH
+
+
+def causal_runs():
+    runs = [(16, 1, list(range(16)) + [DIAGONAL]), (16, 0, [DIAGONAL])]
+    for span in (8, 4, 2, 1):
+        runs.append((span, 1, list(range(span))))
+    return runs
+
+
+def tile_causalexpert_pa_kernel(tc, x_attn, cw1, cb1, cw2, cb2, cln_g, cln_b, out):
+    nc = tc.nc
+    x_rows = x_attn.flatten_outer_dims()
+    out_rows = out.flatten_outer_dims()
+
+    with ExitStack() as ctx:
+        const = ctx.enter_context(tc.tile_pool(name="const", bufs=1))
+        work = ctx.enter_context(tc.tile_pool(name="work", bufs=3))
+        ypool = ctx.enter_context(tc.tile_pool(name="ypool", bufs=10))
+        banks = ctx.enter_context(tc.psum_pool(name="banks", bufs=4))
+        sums = ctx.enter_context(tc.psum_pool(name="sums", bufs=2))
+
+        x_sb = const.tile([P, 2 * GROUPS, WIDTH], BF16)
+        w1_raw = const.tile([P, 2, PACK, WIDTH], BF16)
+        w2_raw = const.tile([P, PACK, WIDTH], BF16)
+        cb1_raw = const.tile([P, PACK], BF16)
+        cb2_raw = const.tile([P, WIDTH], BF16)
+        g_raw = const.tile([P, WIDTH], BF16)
+        b_raw = const.tile([P, WIDTH], BF16)
+
+        def load_x(g):
+            nc.sync.dma_start(
+                out=x_sb[:, 2 * g : 2 * g + 2, :],
+                in_=x_rows[GROUP_ROWS * g : GROUP_ROWS * (g + 1), :].rearrange("(n p) k -> p n k", p=P),
+            )
+
+        load_x(0)
+        for half in range(2):
+            for u in range(2):
+                first_row = WIDTH * half + 2 * P * u
+                nc.sync.dma_start(
+                    out=w1_raw[:, half, 2 * u : 2 * u + 2, :],
+                    in_=cw1[first_row : first_row + 2 * P, :].rearrange("(q e) c -> q e c", e=2),
+                )
+        nc.sync.dma_start(out=cb1_raw[:], in_=cb1.rearrange("(p t) -> p t", t=PACK))
+        nc.sync.dma_start(out=w2_raw[:], in_=cw2.rearrange("(p t) d -> p t d", t=PACK))
+        for g in range(1, GROUPS):
+            load_x(g)
+        nc.sync.dma_start(out=cb2_raw[:], in_=cb2.partition_broadcast(P))
+        nc.sync.dma_start(out=g_raw[:], in_=cln_g.partition_broadcast(P))
+        nc.sync.dma_start(out=b_raw[:], in_=cln_b.partition_broadcast(P))
+
+        ident = const.tile([P, P], F32)
+        make_identity(nc, ident[:])
+        neg_half = const.tile([P, 1], F32)
+        nc.gpsimd.memset(neg_half[:], -0.5)
+        lane = const.tile([P, 1], I32)
+        nc.gpsimd.iota(lane[:], pattern=[[0, 1]], base=0, channel_multiplier=1)
+
+        w1_grp = const.tile([P, 2, WIDTH, PACK], BF16, align_bytes=64)
+        w1_codes = const.tile([P, 2, WIDTH], U32, align_bytes=64)
+        w1_scales = const.tile([P, 2, WIDTH], U8, align_bytes=64)
+        for half in range(2):
+            source = w1_raw[:, half].rearrange("q k (p t) -> q t p k", t=PACK)
+            target = w1_grp[:, half].rearrange("q (t p) k -> q t p k", t=PACK)
+            if half == 0:
+                nc.vector.tensor_copy(out=target, in_=source)
+            else:
+                nc.scalar.copy(out=target, in_=source)
+        for half in range(2):
+            nc.vector.quantize_mx(
+                out=w1_codes[:, half].bitcast(FP8X4),
+                scales=w1_scales[:, half],
+                in_=w1_grp[:, half].rearrange("q c k -> q (c k)"),
+            )
+        cb1_f = const.tile([P, PACK], F32)
+        nc.vector.tensor_copy(out=cb1_f[:], in_=cb1_raw[:])
+
+        w2_grp = const.tile([P, WIDTH, PACK], BF16, align_bytes=64)
+        w2_codes = const.tile([P, WIDTH], U32, align_bytes=64)
+        w2_scales = const.tile([P, WIDTH], U8, align_bytes=64)
+        nc.vector.tensor_copy(out=w2_grp[:], in_=w2_raw[:].rearrange("p t d -> p d t"))
+
+        x_codes = const.tile([P, BATCH * LENGTH], U32, align_bytes=64)
+        x_scales = const.tile([P, BATCH * LENGTH], U8, align_bytes=64)
+        cause = const.tile([P, BATCH * LENGTH, PACK], F32)
+        effect = const.tile([P, BATCH * LENGTH, PACK], F32)
+
+        def project(g):
+            group_rows = slice(GROUP_ROWS * g, GROUP_ROWS * (g + 1))
+            xt = banks.tile([P, 2, 2, P], F32, tag="bank")
+            for n in range(2):
+                words = x_sb[:, 2 * g + n, :].bitcast(F32)
+                for u in range(2):
+                    nc.tensor.transpose(xt[:, n, u, :], words[:, P * u : P * (u + 1)], ident[:])
+            x_grp = work.tile([P, GROUP_ROWS * PACK], BF16, align_bytes=64)
+            nc.vector.tensor_copy(
+                out=x_grp[:].bitcast(F32).rearrange("p (n r u) -> p n r u", n=2, u=2),
+                in_=xt[:].rearrange("p n u r -> p n r u"),
+            )
+            nc.vector.quantize_mx(
+                out=x_codes[:, group_rows].bitcast(FP8X4), scales=x_scales[:, group_rows], in_=x_grp[:]
+            )
+            for half in range(2):
+                for n in range(2):
+                    rows = slice(GROUP_ROWS * g + P * n, GROUP_ROWS * g + P * (n + 1))
+                    bank = banks.tile([P, PACK, P], F32, tag="bank")
+                    for t in range(PACK):
+                        cols = slice(P * t, P * (t + 1))
+                        nc.tensor.matmul_mx(
+                            out=bank[:, t, :],
+                            lhsT=w1_codes[:, half, cols].bitcast(FP8X4),
+                            lhsT_scale=w1_scales[:, half, cols],
+                            rhs=x_codes[:, rows].bitcast(FP8X4),
+                            rhs_scale=x_scales[:, rows],
+                            start=True,
+                            stop=True,
+                        )
+                    by_row = bank[:].rearrange("p t r -> p r t")
+                    if half == 0:
+                        nc.vector.tensor_tensor(
+                            out=cause[:, rows, :],
+                            in0=by_row,
+                            in1=cb1_f[:].unsqueeze(1).to_broadcast([P, P, PACK]),
+                            op=ALU.add,
+                        )
+                    else:
+                        nc.scalar.copy(out=effect[:, rows, :], in_=by_row)
+
+        for g in range(GROUPS):
+            project(g)
+
+        nc.vector.quantize_mx(
+            out=w2_codes[:].bitcast(FP8X4), scales=w2_scales[:], in_=w2_grp[:].rearrange("p d t -> p (d t)")
+        )
+
+        cb2_f = const.tile([P, WIDTH], F32)
+        nc.vector.tensor_copy(out=cb2_f[:], in_=cb2_raw[:])
+        gain = const.tile([P, WIDTH], F32)
+        nc.vector.tensor_scalar_mul(out=gain[:], in0=g_raw[:], scalar1=1.0 / LENGTH)
+        position = const.tile([P, 1], I32)
+        nc.vector.tensor_single_scalar(out=position[:], in_=lane[:], scalar=LENGTH - 1, op=ALU.bitwise_and)
+        share = const.tile([P, 1], F32)
+        nc.vector.tensor_copy(out=share[:], in_=position[:])
+        nc.vector.tensor_scalar(
+            out=share[:], in0=share[:], scalar1=1.0, scalar2=1.0 / LENGTH, op0=ALU.add, op1=ALU.mult
+        )
+        shift = const.tile([P, WIDTH], F32)
+        nc.vector.tensor_scalar_mul(out=shift[:], in0=b_raw[:], scalar1=share[:, 0:1])
+
+        n_tiles = GROUPS * sum(len(effects) for (span, half, effects) in causal_runs())
+        total = const.tile([P, n_tiles], F32)
+        spread = const.tile([P, n_tiles], F32)
+        variance = const.tile([P, n_tiles], F32)
+        rstd = const.tile([P, n_tiles], F32)
+
+        index = 0
+        for g in range(GROUPS):
+            group_rows = slice(GROUP_ROWS * g, GROUP_ROWS * (g + 1))
+            summed = work.tile([P, CHUNKS, GROUP_ROWS], F32, bufs=2)
+            for run, (span, half, effects) in enumerate(causal_runs()):
+                a_blocks = cause[:, group_rows, :].rearrange("p (n h l) t -> p n h l t", h=2, l=span)
+                e_blocks = effect[:, group_rows, :].rearrange("p (n h l) t -> p n h l t", h=2, l=span)
+                n_blocks = GROUP_ROWS // (2 * span)
+                acc = sums.tile([P, CHUNKS, P], F32, tag="acc")
+                for k, eff in enumerate(effects):
+                    col = slice(index, index + 1)
+                    pre = work.tile([P, P * PACK], F32)
+                    if eff == DIAGONAL:
+                        e_view = e_blocks[:, :, half, :, :]
+                    else:
+                        e_view = e_blocks[:, :, 0, eff : eff + 1, :].to_broadcast([P, n_blocks, span, PACK])
+                    nc.vector.tensor_tensor(
+                        out=pre[:].rearrange("p (n l t) -> p n l t", l=span, t=PACK),
+                        in0=a_blocks[:, :, half, :, :],
+                        in1=e_view,
+                        op=ALU.add,
+                    )
+                    h2 = work.tile([P, P * PACK], BF16, align_bytes=64)
+                    nc.scalar.activation(out=h2[:], in_=pre[:], func=ACT.Gelu)
+                    h2_codes = work.tile([P, P], U32, align_bytes=64)
+                    h2_scales = work.tile([P, P], U8, align_bytes=64)
+                    nc.vector.quantize_mx(out=h2_codes[:].bitcast(FP8X4), scales=h2_scales[:], in_=h2[:])
+                    z = banks.tile([P, WIDTH], F32, tag="bank")
+                    nc.tensor.matmul_mx(
+                        out=z[:],
+                        lhsT=h2_codes[:].bitcast(FP8X4),
+                        lhsT_scale=h2_scales[:],
+                        rhs=w2_codes[:].bitcast(FP8X4),
+                        rhs_scale=w2_scales[:],
+                        start=True,
+                        stop=True,
+                    )
+                    y = ypool.tile([P, WIDTH], F32)
+                    nc.vector.scalar_tensor_tensor(
+                        out=y[:], in0=z[:], scalar=1.0, in1=cb2_f[:], op0=ALU.mult, op1=ALU.add,
+                        accum_out=total[:, col],
+                    )
+                    squares = work.tile([P, WIDTH], BF16)
+                    nc.scalar.activation(
+                        out=squares[:], in_=y[:], func=ACT.Square, scale=-float(WIDTH), bias=total[:, col],
+                        accum_out=spread[:, col],
+                    )
+                    nc.gpsimd.tensor_scalar(
+                        out=variance[:, col], in0=spread[:, col], scalar1=1.0 / WIDTH**3, scalar2=EPS,
+                        op0=ALU.mult, op1=ALU.add,
+                    )
+                    nc.gpsimd.tensor_tensor(out=rstd[:, col], in0=variance[:, col], in1=neg_half[:], op=ALU.pow)
+                    if index % 2 == 0:
+                        nc.vector.tensor_scalar_mul(out=y[:], in0=y[:], scalar1=rstd[:, col])
+                    else:
+                        nc.scalar.activation(out=y[:], in_=y[:], func=ACT.Copy, scale=rstd[:, col])
+                    for c in range(CHUNKS):
+                        nc.tensor.matmul(
+                            out=acc[:, c, :],
+                            lhsT=y[:, P * c : P * (c + 1)],
+                            rhs=ident[:],
+                            is_transpose=True,
+                            start=(k == 0 and c == 0),
+                            stop=(k == len(effects) - 1 and c == CHUNKS - 1),
+                        )
+                    index += 1
+                rows_of_run = summed[:].rearrange("p c (n h l) -> p c n h l", h=2, l=span)[:, :, :, half, :]
+                acc_rows = acc[:].rearrange("p c (n l) -> p c n l", l=span)
+                if run < 2:
+                    nc.scalar.copy(out=rows_of_run, in_=acc_rows)
+                else:
+                    nc.vector.tensor_tensor(out=rows_of_run, in0=acc_rows, in1=rows_of_run, op=ALU.add)
+
+            for n in range(GROUP_ROWS // P):
+                back = sums.tile([P, WIDTH], F32, tag="back")
+                for c in range(CHUNKS):
+                    nc.tensor.transpose(back[:, P * c : P * (c + 1)], summed[:, c, P * n : P * (n + 1)], ident[:])
+                raw = work.tile([P, WIDTH], F32)
+                raw_total = work.tile([P, 1], F32)
+                nc.scalar.activation(out=raw[:], in_=back[:], func=ACT.Copy, accum_out=raw_total[:])
+                neg_mean = work.tile([P, 1], F32)
+                nc.vector.tensor_scalar_mul(out=neg_mean[:], in0=raw_total[:], scalar1=-1.0 / WIDTH)
+                result = work.tile([P, WIDTH], F32)
+                nc.vector.scalar_tensor_tensor(
+                    out=result[:], in0=raw[:], scalar=neg_mean[:, 0:1], in1=gain[:], op0=ALU.add, op1=ALU.mult
+                )
+                nc.vector.tensor_tensor(out=result[:], in0=result[:], in1=shift[:], op=ALU.add)
+                first_row = GROUP_ROWS * g + P * n
+                nc.sync.dma_start(out=out_rows[first_row : first_row + P, :], in_=result[:])

@@ -21,6 +21,7 @@ GROUP_BATCH = 8
 GROUPS = BATCH // GROUP_BATCH
 GROUP_ROWS = GROUP_BATCH * LENGTH
 DIAGONAL = -1
+STEP = 4
 
 FLOPS = 2 * BATCH * LENGTH * WIDTH * 2 * WIDTH + 2 * BATCH * (LENGTH * (LENGTH + 1) // 2) * WIDTH * WIDTH
 
@@ -37,12 +38,26 @@ def tile_causalexpert_pa_kernel(tc, x_attn, cw1, cb1, cw2, cb2, cln_g, cln_b, ou
     x_rows = x_attn.flatten_outer_dims()
     out_rows = out.flatten_outer_dims()
 
+    tiles = []
+    for g in range(GROUPS):
+        for span, half, effects in causal_runs():
+            for eff in effects:
+                tiles.append([g, span, half, eff, False, False])
+        tiles[-1][5] = True
+    tiles_per_group = len(tiles) // GROUPS
+    for g in range(GROUPS):
+        tiles[tiles_per_group * g][4] = True
+    n_tiles = len(tiles)
+    n_steps = n_tiles // STEP
+    assert n_steps * STEP == n_tiles
+
     with ExitStack() as ctx:
         const = ctx.enter_context(tc.tile_pool(name="const", bufs=1))
-        work = ctx.enter_context(tc.tile_pool(name="work", bufs=3))
-        ypool = ctx.enter_context(tc.tile_pool(name="ypool", bufs=10))
-        banks = ctx.enter_context(tc.psum_pool(name="banks", bufs=4))
-        sums = ctx.enter_context(tc.psum_pool(name="sums", bufs=2))
+        stream = ctx.enter_context(tc.tile_pool(name="stream", bufs=3))
+        ypool = ctx.enter_context(tc.tile_pool(name="ypool", bufs=4 * STEP))
+        zbanks = ctx.enter_context(tc.psum_pool(name="zbanks", bufs=4))
+        accbanks = ctx.enter_context(tc.psum_pool(name="accbanks", bufs=4))
+        ctx.enter_context(tc.manual_schedule())
 
         x_sb = const.tile([P, 2 * GROUPS, WIDTH], BF16)
         w1_raw = const.tile([P, 2, PACK, WIDTH], BF16)
@@ -76,7 +91,7 @@ def tile_causalexpert_pa_kernel(tc, x_attn, cw1, cb1, cw2, cb2, cln_g, cln_b, ou
 
         ident = const.tile([P, P], F32)
         make_identity(nc, ident[:])
-        neg_half = const.tile([P, 1], F32)
+        neg_half = const.tile([P, STEP], F32)
         nc.gpsimd.memset(neg_half[:], -0.5)
         lane = const.tile([P, 1], I32)
         nc.gpsimd.iota(lane[:], pattern=[[0, 1]], base=0, channel_multiplier=1)
@@ -91,19 +106,14 @@ def tile_causalexpert_pa_kernel(tc, x_attn, cw1, cb1, cw2, cb2, cln_g, cln_b, ou
                 nc.vector.tensor_copy(out=target, in_=source)
             else:
                 nc.scalar.copy(out=target, in_=source)
+        cb1_f = const.tile([P, PACK], F32)
+        nc.vector.tensor_copy(out=cb1_f[:], in_=cb1_raw[:])
         for half in range(2):
             nc.vector.quantize_mx(
                 out=w1_codes[:, half].bitcast(FP8X4),
                 scales=w1_scales[:, half],
                 in_=w1_grp[:, half].rearrange("q c k -> q (c k)"),
             )
-        cb1_f = const.tile([P, PACK], F32)
-        nc.vector.tensor_copy(out=cb1_f[:], in_=cb1_raw[:])
-
-        w2_grp = const.tile([P, WIDTH, PACK], BF16, align_bytes=64)
-        w2_codes = const.tile([P, WIDTH], U32, align_bytes=64)
-        w2_scales = const.tile([P, WIDTH], U8, align_bytes=64)
-        nc.vector.tensor_copy(out=w2_grp[:], in_=w2_raw[:].rearrange("p t d -> p d t"))
 
         x_codes = const.tile([P, BATCH * LENGTH], U32, align_bytes=64)
         x_scales = const.tile([P, BATCH * LENGTH], U8, align_bytes=64)
@@ -112,12 +122,12 @@ def tile_causalexpert_pa_kernel(tc, x_attn, cw1, cb1, cw2, cb2, cln_g, cln_b, ou
 
         def project(g):
             group_rows = slice(GROUP_ROWS * g, GROUP_ROWS * (g + 1))
-            xt = banks.tile([P, 2, 2, P], F32, tag="bank")
+            xt = accbanks.tile([P, 2, 2, P], F32, tag="acc")
             for n in range(2):
                 words = x_sb[:, 2 * g + n, :].bitcast(F32)
                 for u in range(2):
                     nc.tensor.transpose(xt[:, n, u, :], words[:, P * u : P * (u + 1)], ident[:])
-            x_grp = work.tile([P, GROUP_ROWS * PACK], BF16, align_bytes=64)
+            x_grp = stream.tile([P, GROUP_ROWS * PACK], BF16, align_bytes=64)
             nc.vector.tensor_copy(
                 out=x_grp[:].bitcast(F32).rearrange("p (n r u) -> p n r u", n=2, u=2),
                 in_=xt[:].rearrange("p n u r -> p n r u"),
@@ -125,10 +135,10 @@ def tile_causalexpert_pa_kernel(tc, x_attn, cw1, cb1, cw2, cb2, cln_g, cln_b, ou
             nc.vector.quantize_mx(
                 out=x_codes[:, group_rows].bitcast(FP8X4), scales=x_scales[:, group_rows], in_=x_grp[:]
             )
-            for half in range(2):
-                for n in range(2):
+            for n in range(2):
+                for half in range(2):
                     rows = slice(GROUP_ROWS * g + P * n, GROUP_ROWS * g + P * (n + 1))
-                    bank = banks.tile([P, PACK, P], F32, tag="bank")
+                    bank = accbanks.tile([P, PACK, P], F32, tag="acc")
                     for t in range(PACK):
                         cols = slice(P * t, P * (t + 1))
                         nc.tensor.matmul_mx(
@@ -151,119 +161,212 @@ def tile_causalexpert_pa_kernel(tc, x_attn, cw1, cb1, cw2, cb2, cln_g, cln_b, ou
                     else:
                         nc.scalar.copy(out=effect[:, rows, :], in_=by_row)
 
-        for g in range(GROUPS):
-            project(g)
+        project(0)
 
-        nc.vector.quantize_mx(
-            out=w2_codes[:].bitcast(FP8X4), scales=w2_scales[:], in_=w2_grp[:].rearrange("p d t -> p (d t)")
-        )
-
+        w2_grp = const.tile([P, WIDTH, PACK], BF16, align_bytes=64)
+        w2_codes = const.tile([P, WIDTH], U32, align_bytes=64)
+        w2_scales = const.tile([P, WIDTH], U8, align_bytes=64)
         cb2_f = const.tile([P, WIDTH], F32)
-        nc.vector.tensor_copy(out=cb2_f[:], in_=cb2_raw[:])
         gain = const.tile([P, WIDTH], F32)
-        nc.vector.tensor_scalar_mul(out=gain[:], in0=g_raw[:], scalar1=1.0 / LENGTH)
-        position = const.tile([P, 1], I32)
-        nc.vector.tensor_single_scalar(out=position[:], in_=lane[:], scalar=LENGTH - 1, op=ALU.bitwise_and)
-        share = const.tile([P, 1], F32)
-        nc.vector.tensor_copy(out=share[:], in_=position[:])
-        nc.vector.tensor_scalar(
-            out=share[:], in0=share[:], scalar1=1.0, scalar2=1.0 / LENGTH, op0=ALU.add, op1=ALU.mult
-        )
         shift = const.tile([P, WIDTH], F32)
-        nc.vector.tensor_scalar_mul(out=shift[:], in0=b_raw[:], scalar1=share[:, 0:1])
+        position = const.tile([P, 1], I32)
+        share = const.tile([P, 1], F32)
 
-        n_tiles = GROUPS * sum(len(effects) for (span, half, effects) in causal_runs())
+        def prepare_second_half():
+            nc.vector.tensor_copy(out=w2_grp[:], in_=w2_raw[:].rearrange("p t d -> p d t"))
+            nc.vector.tensor_copy(out=cb2_f[:], in_=cb2_raw[:])
+            nc.vector.quantize_mx(
+                out=w2_codes[:].bitcast(FP8X4), scales=w2_scales[:], in_=w2_grp[:].rearrange("p d t -> p (d t)")
+            )
+            nc.vector.tensor_scalar_mul(out=gain[:], in0=g_raw[:], scalar1=1.0 / LENGTH)
+            nc.vector.tensor_single_scalar(out=position[:], in_=lane[:], scalar=LENGTH - 1, op=ALU.bitwise_and)
+            nc.vector.tensor_copy(out=share[:], in_=position[:])
+            nc.vector.tensor_scalar(
+                out=share[:], in0=share[:], scalar1=1.0, scalar2=1.0 / LENGTH, op0=ALU.add, op1=ALU.mult
+            )
+            nc.vector.tensor_scalar_mul(out=shift[:], in0=b_raw[:], scalar1=share[:, 0:1])
+
         total = const.tile([P, n_tiles], F32)
         spread = const.tile([P, n_tiles], F32)
         variance = const.tile([P, n_tiles], F32)
         rstd = const.tile([P, n_tiles], F32)
+        pre_of, h2_of, codes_of, scales_of, z_of, y_of, acc_of, summed_of, back_of, raw_of = (
+            {}, {}, {}, {}, {}, {}, {}, {}, {}, {},
+        )
 
-        index = 0
-        for g in range(GROUPS):
-            group_rows = slice(GROUP_ROWS * g, GROUP_ROWS * (g + 1))
-            summed = work.tile([P, CHUNKS, GROUP_ROWS], F32, bufs=2)
-            for run, (span, half, effects) in enumerate(causal_runs()):
+        def add(s):
+            pre = stream.tile([P, STEP, P * PACK], F32)
+            pre_of[s] = pre
+            for k in range(STEP):
+                g, span, half, eff, first, last = tiles[STEP * s + k]
+                group_rows = slice(GROUP_ROWS * g, GROUP_ROWS * (g + 1))
                 a_blocks = cause[:, group_rows, :].rearrange("p (n h l) t -> p n h l t", h=2, l=span)
                 e_blocks = effect[:, group_rows, :].rearrange("p (n h l) t -> p n h l t", h=2, l=span)
-                n_blocks = GROUP_ROWS // (2 * span)
-                acc = sums.tile([P, CHUNKS, P], F32, tag="acc")
-                for k, eff in enumerate(effects):
-                    col = slice(index, index + 1)
-                    pre = work.tile([P, P * PACK], F32)
-                    if eff == DIAGONAL:
-                        e_view = e_blocks[:, :, half, :, :]
-                    else:
-                        e_view = e_blocks[:, :, 0, eff : eff + 1, :].to_broadcast([P, n_blocks, span, PACK])
-                    nc.vector.tensor_tensor(
-                        out=pre[:].rearrange("p (n l t) -> p n l t", l=span, t=PACK),
-                        in0=a_blocks[:, :, half, :, :],
-                        in1=e_view,
-                        op=ALU.add,
-                    )
-                    h2 = work.tile([P, P * PACK], BF16, align_bytes=64)
-                    nc.scalar.activation(out=h2[:], in_=pre[:], func=ACT.Gelu)
-                    h2_codes = work.tile([P, P], U32, align_bytes=64)
-                    h2_scales = work.tile([P, P], U8, align_bytes=64)
-                    nc.vector.quantize_mx(out=h2_codes[:].bitcast(FP8X4), scales=h2_scales[:], in_=h2[:])
-                    z = banks.tile([P, WIDTH], F32, tag="bank")
-                    nc.tensor.matmul_mx(
-                        out=z[:],
-                        lhsT=h2_codes[:].bitcast(FP8X4),
-                        lhsT_scale=h2_scales[:],
-                        rhs=w2_codes[:].bitcast(FP8X4),
-                        rhs_scale=w2_scales[:],
-                        start=True,
-                        stop=True,
-                    )
-                    y = ypool.tile([P, WIDTH], F32)
-                    nc.vector.scalar_tensor_tensor(
-                        out=y[:], in0=z[:], scalar=1.0, in1=cb2_f[:], op0=ALU.mult, op1=ALU.add,
-                        accum_out=total[:, col],
-                    )
-                    squares = work.tile([P, WIDTH], BF16)
-                    nc.scalar.activation(
-                        out=squares[:], in_=y[:], func=ACT.Square, scale=-float(WIDTH), bias=total[:, col],
-                        accum_out=spread[:, col],
-                    )
-                    nc.gpsimd.tensor_scalar(
-                        out=variance[:, col], in0=spread[:, col], scalar1=1.0 / WIDTH**3, scalar2=EPS,
-                        op0=ALU.mult, op1=ALU.add,
-                    )
-                    nc.gpsimd.tensor_tensor(out=rstd[:, col], in0=variance[:, col], in1=neg_half[:], op=ALU.pow)
-                    if index % 2 == 0:
-                        nc.vector.tensor_scalar_mul(out=y[:], in0=y[:], scalar1=rstd[:, col])
-                    else:
-                        nc.scalar.activation(out=y[:], in_=y[:], func=ACT.Copy, scale=rstd[:, col])
-                    for c in range(CHUNKS):
-                        nc.tensor.matmul(
-                            out=acc[:, c, :],
-                            lhsT=y[:, P * c : P * (c + 1)],
-                            rhs=ident[:],
-                            is_transpose=True,
-                            start=(k == 0 and c == 0),
-                            stop=(k == len(effects) - 1 and c == CHUNKS - 1),
-                        )
-                    index += 1
-                rows_of_run = summed[:].rearrange("p c (n h l) -> p c n h l", h=2, l=span)[:, :, :, half, :]
-                acc_rows = acc[:].rearrange("p c (n l) -> p c n l", l=span)
-                if run < 2:
-                    nc.scalar.copy(out=rows_of_run, in_=acc_rows)
+                if eff == DIAGONAL:
+                    e_view = e_blocks[:, :, half, :, :]
                 else:
-                    nc.vector.tensor_tensor(out=rows_of_run, in0=acc_rows, in1=rows_of_run, op=ALU.add)
+                    e_view = e_blocks[:, :, 0, eff : eff + 1, :].to_broadcast(
+                        [P, GROUP_ROWS // (2 * span), span, PACK]
+                    )
+                nc.vector.tensor_tensor(
+                    out=pre[:, k, :].rearrange("p (n l t) -> p n l t", l=span, t=PACK),
+                    in0=a_blocks[:, :, half, :, :],
+                    in1=e_view,
+                    op=ALU.add,
+                )
 
-            for n in range(GROUP_ROWS // P):
-                back = sums.tile([P, WIDTH], F32, tag="back")
+        def gelu(s):
+            h2 = stream.tile([P, STEP * P * PACK], BF16, align_bytes=64)
+            h2_of[s] = h2
+            nc.scalar.activation(out=h2[:], in_=pre_of[s][:].rearrange("p k m -> p (k m)"), func=ACT.Gelu)
+
+        def quantise(s):
+            h2_codes = stream.tile([P, STEP * P], U32, align_bytes=64)
+            h2_scales = stream.tile([P, STEP * P], U8, align_bytes=64)
+            codes_of[s], scales_of[s] = h2_codes, h2_scales
+            nc.vector.quantize_mx(out=h2_codes[:].bitcast(FP8X4), scales=h2_scales[:], in_=h2_of[s][:])
+
+        def product(s):
+            for k in range(STEP):
+                z = zbanks.tile([P, WIDTH], F32)
+                z_of[STEP * s + k] = z
+                pairs = slice(P * k, P * (k + 1))
+                nc.tensor.matmul_mx(
+                    out=z[:],
+                    lhsT=codes_of[s][:, pairs].bitcast(FP8X4),
+                    lhsT_scale=scales_of[s][:, pairs],
+                    rhs=w2_codes[:].bitcast(FP8X4),
+                    rhs_scale=w2_scales[:],
+                    start=True,
+                    stop=True,
+                )
+
+        def bias(s):
+            for index in range(STEP * s, STEP * (s + 1)):
+                y = ypool.tile([P, WIDTH], F32)
+                y_of[index] = y
+                nc.vector.scalar_tensor_tensor(
+                    out=y[:], in0=z_of[index][:], scalar=1.0, in1=cb2_f[:], op0=ALU.mult, op1=ALU.add,
+                    accum_out=total[:, index : index + 1],
+                )
+
+        def deviation(s):
+            for index in range(STEP * s, STEP * (s + 1)):
+                squares = stream.tile([P, WIDTH], BF16)
+                nc.scalar.activation(
+                    out=squares[:], in_=y_of[index][:], func=ACT.Square, scale=-float(WIDTH),
+                    bias=total[:, index : index + 1], accum_out=spread[:, index : index + 1],
+                )
+            cols = slice(STEP * s, STEP * (s + 1))
+            nc.gpsimd.tensor_scalar(
+                out=variance[:, cols], in0=spread[:, cols], scalar1=1.0 / WIDTH**3, scalar2=EPS,
+                op0=ALU.mult, op1=ALU.add,
+            )
+            nc.gpsimd.tensor_tensor(out=rstd[:, cols], in0=variance[:, cols], in1=neg_half[:], op=ALU.pow)
+
+        def scale(s):
+            for index in range(STEP * s, STEP * (s + 1)):
+                y = y_of[index]
+                if index % 2 == 0:
+                    nc.vector.tensor_scalar_mul(out=y[:], in0=y[:], scalar1=rstd[:, index : index + 1])
+                else:
+                    nc.scalar.activation(out=y[:], in_=y[:], func=ACT.Copy, scale=rstd[:, index : index + 1])
+
+        def sum_up(s):
+            for index in range(STEP * s, STEP * (s + 1)):
+                g, span, half, eff, first, last = tiles[index]
+                if first:
+                    acc_lo = accbanks.tile([P, 2, GROUP_ROWS], F32, tag="acc")
+                    acc_hi = accbanks.tile([P, 2, GROUP_ROWS], F32, tag="acc")
+                    acc_of[g] = (acc_lo, acc_hi)
                 for c in range(CHUNKS):
-                    nc.tensor.transpose(back[:, P * c : P * (c + 1)], summed[:, c, P * n : P * (n + 1)], ident[:])
-                raw = work.tile([P, WIDTH], F32)
-                raw_total = work.tile([P, 1], F32)
-                nc.scalar.activation(out=raw[:], in_=back[:], func=ACT.Copy, accum_out=raw_total[:])
-                neg_mean = work.tile([P, 1], F32)
+                    columns = acc_of[g][c // 2][:, c % 2, :].rearrange("p (n h l) -> p n h l", h=2, l=span)
+                    nc.tensor.matmul(
+                        out=columns[:, :, half, :],
+                        lhsT=y_of[index][:, P * c : P * (c + 1)],
+                        rhs=ident[:].rearrange("p (n l) -> p n l", l=span),
+                        is_transpose=True,
+                        start=(first and c % 2 == 0),
+                        stop=(last and c % 2 == 1),
+                    )
+
+        def group_ending_in(s):
+            for g in range(GROUPS):
+                if (tiles_per_group * (g + 1) - 1) // STEP == s:
+                    return g
+            return None
+
+        def unload(s):
+            g = group_ending_in(s)
+            if g is None:
+                return
+            summed = stream.tile([P, CHUNKS, GROUP_ROWS], F32, bufs=2)
+            summed_of[g] = summed
+            nc.scalar.copy(out=summed[:, 0:2, :], in_=acc_of[g][0][:])
+            nc.vector.tensor_copy(out=summed[:, 2:4, :], in_=acc_of[g][1][:])
+
+        def turn_back(s):
+            g = group_ending_in(s)
+            if g is None:
+                return
+            for n in range(GROUP_ROWS // P):
+                back = accbanks.tile([P, WIDTH], F32, tag="acc")
+                back_of[(g, n)] = back
+                for c in range(CHUNKS):
+                    nc.tensor.transpose(
+                        back[:, P * c : P * (c + 1)], summed_of[g][:, c, P * n : P * (n + 1)], ident[:]
+                    )
+
+        def centre(s):
+            g = group_ending_in(s)
+            if g is None:
+                return
+            for n in range(GROUP_ROWS // P):
+                raw = stream.tile([P, WIDTH], F32, bufs=2)
+                raw_total = stream.tile([P, 1], F32, bufs=2)
+                raw_of[(g, n)] = (raw, raw_total)
+                nc.scalar.activation(out=raw[:], in_=back_of[(g, n)][:], func=ACT.Copy, accum_out=raw_total[:])
+
+        def affine(s):
+            g = group_ending_in(s)
+            if g is None:
+                return
+            for n in range(GROUP_ROWS // P):
+                raw, raw_total = raw_of[(g, n)]
+                neg_mean = stream.tile([P, 1], F32, bufs=2)
                 nc.vector.tensor_scalar_mul(out=neg_mean[:], in0=raw_total[:], scalar1=-1.0 / WIDTH)
-                result = work.tile([P, WIDTH], F32)
+                result = stream.tile([P, WIDTH], F32, bufs=2)
                 nc.vector.scalar_tensor_tensor(
                     out=result[:], in0=raw[:], scalar=neg_mean[:, 0:1], in1=gain[:], op0=ALU.add, op1=ALU.mult
                 )
                 nc.vector.tensor_tensor(out=result[:], in0=result[:], in1=shift[:], op=ALU.add)
                 first_row = GROUP_ROWS * g + P * n
                 nc.sync.dma_start(out=out_rows[first_row : first_row + P, :], in_=result[:])
+
+        def in_range(s):
+            return 0 <= s < n_steps
+
+        for now in range(n_steps + 11):
+            if in_range(now - 6):
+                sum_up(now - 6)
+            if in_range(now - 2):
+                quantise(now - 2)
+                product(now - 2)
+            if in_range(now - 3):
+                bias(now - 3)
+            if in_range(now - 1):
+                gelu(now - 1)
+            if in_range(now - 4):
+                deviation(now - 4)
+            if in_range(now):
+                add(now)
+            if in_range(now - 5):
+                scale(now - 5)
+            unload(now - 7)
+            turn_back(now - 8)
+            centre(now - 9)
+            affine(now - 10)
+            if now == 0:
+                prepare_second_half()
+            if now + 1 < GROUPS:
+                project(now + 1)

@@ -22,6 +22,8 @@ GROUPS = BATCH // GROUP_BATCH
 GROUP_ROWS = GROUP_BATCH * LENGTH
 DIAGONAL = -1
 STEP = 4
+GPSIMD_ADDS = 1
+SCALAR_SCALES = 1
 
 FLOPS = 2 * BATCH * LENGTH * WIDTH * 2 * WIDTH + 2 * BATCH * (LENGTH * (LENGTH + 1) // 2) * WIDTH * WIDTH
 
@@ -208,7 +210,8 @@ def tile_causalexpert_pa_kernel(tc, x_attn, cw1, cb1, cw2, cb2, cln_g, cln_b, ou
                     e_view = e_blocks[:, :, 0, eff : eff + 1, :].to_broadcast(
                         [P, GROUP_ROWS // (2 * span), span, PACK]
                     )
-                nc.vector.tensor_tensor(
+                adder = nc.gpsimd if k >= STEP - GPSIMD_ADDS else nc.vector
+                adder.tensor_tensor(
                     out=pre[:, k, :].rearrange("p (n l t) -> p n l t", l=span, t=PACK),
                     in0=a_blocks[:, :, half, :, :],
                     in1=e_view,
@@ -267,7 +270,7 @@ def tile_causalexpert_pa_kernel(tc, x_attn, cw1, cb1, cw2, cb2, cln_g, cln_b, ou
         def scale(s):
             for index in range(STEP * s, STEP * (s + 1)):
                 y = y_of[index]
-                if index % 2 == 0:
+                if index % STEP < STEP - SCALAR_SCALES:
                     nc.vector.tensor_scalar_mul(out=y[:], in0=y[:], scalar1=rstd[:, index : index + 1])
                 else:
                     nc.scalar.activation(out=y[:], in_=y[:], func=ACT.Copy, scale=rstd[:, index : index + 1])

@@ -22,8 +22,8 @@ GROUPS = BATCH // GROUP_BATCH
 GROUP_ROWS = GROUP_BATCH * LENGTH
 DIAGONAL = -1
 STEP = 4
-GPSIMD_ADDS = 1
-SCALAR_SCALES = 1
+GPSIMD_ADDS = 2
+SCALAR_SCALES = 2
 
 FLOPS = 2 * BATCH * LENGTH * WIDTH * 2 * WIDTH + 2 * BATCH * (LENGTH * (LENGTH + 1) // 2) * WIDTH * WIDTH
 
@@ -359,10 +359,10 @@ def tile_causalexpert_pa_kernel(tc, x_attn, cw1, cb1, cw2, cb2, cln_g, cln_b, ou
                 bias(now - 3)
             if in_range(now - 1):
                 gelu(now - 1)
-            if in_range(now - 4):
-                deviation(now - 4)
             if in_range(now):
                 add(now)
+            if in_range(now - 4):
+                deviation(now - 4)
             if in_range(now - 5):
                 scale(now - 5)
             unload(now - 7)

@@ -23,7 +23,7 @@ GROUP_ROWS = GROUP_BATCH * LENGTH
 DIAGONAL = -1
 STEP = 4
 GPSIMD_ADDS = 2
-SCALAR_SCALES = 2
+SCALAR_SCALES = 1
 
 FLOPS = 2 * BATCH * LENGTH * WIDTH * 2 * WIDTH + 2 * BATCH * (LENGTH * (LENGTH + 1) // 2) * WIDTH * WIDTH
 
@@ -83,10 +83,10 @@ def tile_causalexpert_pa_kernel(tc, x_attn, cw1, cb1, cw2, cb2, cln_g, cln_b, ou
                     out=w1_raw[:, half, 2 * u : 2 * u + 2, :],
                     in_=cw1[first_row : first_row + 2 * P, :].rearrange("(q e) c -> q e c", e=2),
                 )
-        nc.sync.dma_start(out=cb1_raw[:], in_=cb1.rearrange("(p t) -> p t", t=PACK))
-        nc.sync.dma_start(out=w2_raw[:], in_=cw2.rearrange("(p t) d -> p t d", t=PACK))
         for g in range(1, GROUPS):
             load_x(g)
+        nc.sync.dma_start(out=cb1_raw[:], in_=cb1.rearrange("(p t) -> p t", t=PACK))
+        nc.sync.dma_start(out=w2_raw[:], in_=cw2.rearrange("(p t) d -> p t d", t=PACK))
         nc.sync.dma_start(out=cb2_raw[:], in_=cb2.partition_broadcast(P))
         nc.sync.dma_start(out=g_raw[:], in_=cln_g.partition_broadcast(P))
         nc.sync.dma_start(out=b_raw[:], in_=cln_b.partition_broadcast(P))
@@ -98,45 +98,86 @@ def tile_causalexpert_pa_kernel(tc, x_attn, cw1, cb1, cw2, cb2, cln_g, cln_b, ou
         lane = const.tile([P, 1], I32)
         nc.gpsimd.iota(lane[:], pattern=[[0, 1]], base=0, channel_multiplier=1)
 
+        x_grp = const.tile([P, BATCH * LENGTH * PACK], BF16, align_bytes=64)
+        x_codes = const.tile([P, BATCH * LENGTH], U32, align_bytes=64)
+        x_scales = const.tile([P, BATCH * LENGTH], U8, align_bytes=64)
         w1_grp = const.tile([P, 2, WIDTH, PACK], BF16, align_bytes=64)
         w1_codes = const.tile([P, 2, WIDTH], U32, align_bytes=64)
         w1_scales = const.tile([P, 2, WIDTH], U8, align_bytes=64)
-        for half in range(2):
-            source = w1_raw[:, half].rearrange("q k (p t) -> q t p k", t=PACK)
-            target = w1_grp[:, half].rearrange("q (t p) k -> q t p k", t=PACK)
-            if half == 0:
-                nc.vector.tensor_copy(out=target, in_=source)
-            else:
-                nc.scalar.copy(out=target, in_=source)
-        cb1_f = const.tile([P, PACK], F32)
-        nc.vector.tensor_copy(out=cb1_f[:], in_=cb1_raw[:])
-        for half in range(2):
+        w2_grp = const.tile([P, WIDTH, PACK], BF16, align_bytes=64)
+        w2_codes = const.tile([P, WIDTH], U32, align_bytes=64)
+        w2_scales = const.tile([P, WIDTH], U8, align_bytes=64)
+
+        def turn_x(g):
+            xt = accbanks.tile([P, 2, 2, P], F32, tag="acc")
+            for n in range(2):
+                words = x_sb[:, 2 * g + n, :].bitcast(F32)
+                for u in range(2):
+                    nc.tensor.transpose(xt[:, n, u, :], words[:, P * u : P * (u + 1)], ident[:])
+            nc.scalar.copy(
+                out=x_grp[:, GROUP_ROWS * PACK * g : GROUP_ROWS * PACK * (g + 1)]
+                .bitcast(F32)
+                .rearrange("p (n r u) -> p n r u", n=2, u=2),
+                in_=xt[:].rearrange("p n u r -> p n r u"),
+            )
+
+        def quantise_x(g):
+            group_rows = slice(GROUP_ROWS * g, GROUP_ROWS * (g + 1))
+            nc.vector.quantize_mx(
+                out=x_codes[:, group_rows].bitcast(FP8X4),
+                scales=x_scales[:, group_rows],
+                in_=x_grp[:, GROUP_ROWS * PACK * g : GROUP_ROWS * PACK * (g + 1)],
+            )
+
+        def regroup_w1(half, engine_copy):
+            engine_copy(
+                out=w1_grp[:, half].rearrange("q (t p) k -> q t p k", t=PACK),
+                in_=w1_raw[:, half].rearrange("q k (p t) -> q t p k", t=PACK),
+            )
+
+        def quantise_w1(half):
             nc.vector.quantize_mx(
                 out=w1_codes[:, half].bitcast(FP8X4),
                 scales=w1_scales[:, half],
                 in_=w1_grp[:, half].rearrange("q c k -> q (c k)"),
             )
 
-        x_codes = const.tile([P, BATCH * LENGTH], U32, align_bytes=64)
-        x_scales = const.tile([P, BATCH * LENGTH], U8, align_bytes=64)
+        turn_x(0)
+        regroup_w1(0, nc.vector.tensor_copy)
+        regroup_w1(1, nc.scalar.copy)
+        for g in range(1, GROUPS):
+            turn_x(g)
+        nc.scalar.copy(out=w2_grp[:], in_=w2_raw[:].rearrange("p t d -> p d t"))
+        quantise_x(0)
+        quantise_w1(0)
+        cb1_f = const.tile([P, PACK], F32)
+        nc.vector.tensor_copy(out=cb1_f[:], in_=cb1_raw[:])
+        position = const.tile([P, 1], I32)
+        share = const.tile([P, 1], F32)
+        nc.vector.tensor_single_scalar(out=position[:], in_=lane[:], scalar=LENGTH - 1, op=ALU.bitwise_and)
+        nc.vector.tensor_copy(out=share[:], in_=position[:])
+        nc.vector.tensor_scalar(
+            out=share[:], in0=share[:], scalar1=1.0, scalar2=1.0 / LENGTH, op0=ALU.add, op1=ALU.mult
+        )
+        quantise_w1(1)
+        for g in range(1, GROUPS):
+            quantise_x(g)
+
+        cb2_f = const.tile([P, WIDTH], F32)
+        gain = const.tile([P, WIDTH], F32)
+        shift = const.tile([P, WIDTH], F32)
+        nc.gpsimd.tensor_scalar(out=cb2_f[:], in0=cb2_raw[:], scalar1=1.0, scalar2=0.0, op0=ALU.mult, op1=ALU.add)
+        nc.gpsimd.tensor_scalar(
+            out=gain[:], in0=g_raw[:], scalar1=1.0 / LENGTH, scalar2=0.0, op0=ALU.mult, op1=ALU.add
+        )
+        nc.gpsimd.tensor_scalar(
+            out=shift[:], in0=b_raw[:], scalar1=share[:, 0:1], scalar2=0.0, op0=ALU.mult, op1=ALU.add
+        )
+
         cause = const.tile([P, BATCH * LENGTH, PACK], F32)
         effect = const.tile([P, BATCH * LENGTH, PACK], F32)
 
         def project(g):
-            group_rows = slice(GROUP_ROWS * g, GROUP_ROWS * (g + 1))
-            xt = accbanks.tile([P, 2, 2, P], F32, tag="acc")
-            for n in range(2):
-                words = x_sb[:, 2 * g + n, :].bitcast(F32)
-                for u in range(2):
-                    nc.tensor.transpose(xt[:, n, u, :], words[:, P * u : P * (u + 1)], ident[:])
-            x_grp = stream.tile([P, GROUP_ROWS * PACK], BF16, align_bytes=64)
-            nc.vector.tensor_copy(
-                out=x_grp[:].bitcast(F32).rearrange("p (n r u) -> p n r u", n=2, u=2),
-                in_=xt[:].rearrange("p n u r -> p n r u"),
-            )
-            nc.vector.quantize_mx(
-                out=x_codes[:, group_rows].bitcast(FP8X4), scales=x_scales[:, group_rows], in_=x_grp[:]
-            )
             for n in range(2):
                 for half in range(2):
                     rows = slice(GROUP_ROWS * g + P * n, GROUP_ROWS * g + P * (n + 1))
@@ -164,29 +205,6 @@ def tile_causalexpert_pa_kernel(tc, x_attn, cw1, cb1, cw2, cb2, cln_g, cln_b, ou
                         nc.scalar.copy(out=effect[:, rows, :], in_=by_row)
 
         project(0)
-
-        w2_grp = const.tile([P, WIDTH, PACK], BF16, align_bytes=64)
-        w2_codes = const.tile([P, WIDTH], U32, align_bytes=64)
-        w2_scales = const.tile([P, WIDTH], U8, align_bytes=64)
-        cb2_f = const.tile([P, WIDTH], F32)
-        gain = const.tile([P, WIDTH], F32)
-        shift = const.tile([P, WIDTH], F32)
-        position = const.tile([P, 1], I32)
-        share = const.tile([P, 1], F32)
-
-        def prepare_second_half():
-            nc.vector.tensor_copy(out=w2_grp[:], in_=w2_raw[:].rearrange("p t d -> p d t"))
-            nc.vector.tensor_copy(out=cb2_f[:], in_=cb2_raw[:])
-            nc.vector.quantize_mx(
-                out=w2_codes[:].bitcast(FP8X4), scales=w2_scales[:], in_=w2_grp[:].rearrange("p d t -> p (d t)")
-            )
-            nc.vector.tensor_scalar_mul(out=gain[:], in0=g_raw[:], scalar1=1.0 / LENGTH)
-            nc.vector.tensor_single_scalar(out=position[:], in_=lane[:], scalar=LENGTH - 1, op=ALU.bitwise_and)
-            nc.vector.tensor_copy(out=share[:], in_=position[:])
-            nc.vector.tensor_scalar(
-                out=share[:], in0=share[:], scalar1=1.0, scalar2=1.0 / LENGTH, op0=ALU.add, op1=ALU.mult
-            )
-            nc.vector.tensor_scalar_mul(out=shift[:], in0=b_raw[:], scalar1=share[:, 0:1])
 
         total = const.tile([P, n_tiles], F32)
         spread = const.tile([P, n_tiles], F32)
@@ -370,6 +388,8 @@ def tile_causalexpert_pa_kernel(tc, x_attn, cw1, cb1, cw2, cb2, cln_g, cln_b, ou
             centre(now - 9)
             affine(now - 10)
             if now == 0:
-                prepare_second_half()
+                nc.vector.quantize_mx(
+                    out=w2_codes[:].bitcast(FP8X4), scales=w2_scales[:], in_=w2_grp[:].rearrange("p d t -> p (d t)")
+                )
             if now + 1 < GROUPS:
                 project(now + 1)

@@ -22,8 +22,8 @@ GROUPS = BATCH // GROUP_BATCH
 GROUP_ROWS = GROUP_BATCH * LENGTH
 DIAGONAL = -1
 STEP = 4
-GPSIMD_ADDS = 2
-SCALAR_SCALES = 1
+GPSIMD_ADDS = 1
+SCALAR_SCALES = 2
 
 FLOPS = 2 * BATCH * LENGTH * WIDTH * 2 * WIDTH + 2 * BATCH * (LENGTH * (LENGTH + 1) // 2) * WIDTH * WIDTH
 

@@ -15,17 +15,19 @@ ACT = mybir.ActivationFunctionType
 P = 128
 PACK = 4
 BATCH, LENGTH, WIDTH = 32, 32, 512
+ROWS = BATCH * LENGTH
 EPS = 1e-5
 CHUNKS = WIDTH // P
 GROUP_BATCH = 8
 GROUPS = BATCH // GROUP_BATCH
 GROUP_ROWS = GROUP_BATCH * LENGTH
+ROW_TILES = GROUP_ROWS // P
 DIAGONAL = -1
 STEP = 4
 GPSIMD_ADDS = 1
-SCALAR_SCALES = 2
+SCALAR_SCALES = 1
 
-FLOPS = 2 * BATCH * LENGTH * WIDTH * 2 * WIDTH + 2 * BATCH * (LENGTH * (LENGTH + 1) // 2) * WIDTH * WIDTH
+FLOPS = 2 * ROWS * WIDTH * 2 * WIDTH + 2 * BATCH * (LENGTH * (LENGTH + 1) // 2) * WIDTH * WIDTH
 
 
 def causal_runs():
@@ -44,12 +46,9 @@ def tile_causalexpert_pa_kernel(tc, x_attn, cw1, cb1, cw2, cb2, cln_g, cln_b, ou
     for g in range(GROUPS):
         for span, half, effects in causal_runs():
             for eff in effects:
-                tiles.append([g, span, half, eff, False, False])
-        tiles[-1][5] = True
-    tiles_per_group = len(tiles) // GROUPS
-    for g in range(GROUPS):
-        tiles[tiles_per_group * g][4] = True
+                tiles.append((g, span, half, eff))
     n_tiles = len(tiles)
+    tiles_per_group = n_tiles // GROUPS
     n_steps = n_tiles // STEP
     assert n_steps * STEP == n_tiles
 
@@ -57,11 +56,11 @@ def tile_causalexpert_pa_kernel(tc, x_attn, cw1, cb1, cw2, cb2, cln_g, cln_b, ou
         const = ctx.enter_context(tc.tile_pool(name="const", bufs=1))
         stream = ctx.enter_context(tc.tile_pool(name="stream", bufs=3))
         ypool = ctx.enter_context(tc.tile_pool(name="ypool", bufs=4 * STEP))
-        zbanks = ctx.enter_context(tc.psum_pool(name="zbanks", bufs=4))
+        zbanks = ctx.enter_context(tc.psum_pool(name="zbanks", bufs=STEP))
         accbanks = ctx.enter_context(tc.psum_pool(name="accbanks", bufs=4))
         ctx.enter_context(tc.manual_schedule())
 
-        x_sb = const.tile([P, 2 * GROUPS, WIDTH], BF16)
+        x_sb = const.tile([P, ROW_TILES * GROUPS, WIDTH], BF16)
         w1_raw = const.tile([P, 2, PACK, WIDTH], BF16)
         w2_raw = const.tile([P, PACK, WIDTH], BF16)
         cb1_raw = const.tile([P, PACK], BF16)
@@ -71,7 +70,7 @@ def tile_causalexpert_pa_kernel(tc, x_attn, cw1, cb1, cw2, cb2, cln_g, cln_b, ou
 
         def load_x(g):
             nc.sync.dma_start(
-                out=x_sb[:, 2 * g : 2 * g + 2, :],
+                out=x_sb[:, ROW_TILES * g : ROW_TILES * (g + 1), :],
                 in_=x_rows[GROUP_ROWS * g : GROUP_ROWS * (g + 1), :].rearrange("(n p) k -> p n k", p=P),
             )
 
@@ -98,9 +97,9 @@ def tile_causalexpert_pa_kernel(tc, x_attn, cw1, cb1, cw2, cb2, cln_g, cln_b, ou
         lane = const.tile([P, 1], I32)
         nc.gpsimd.iota(lane[:], pattern=[[0, 1]], base=0, channel_multiplier=1)
 
-        x_grp = const.tile([P, BATCH * LENGTH * PACK], BF16, align_bytes=64)
-        x_codes = const.tile([P, BATCH * LENGTH], U32, align_bytes=64)
-        x_scales = const.tile([P, BATCH * LENGTH], U8, align_bytes=64)
+        x_grp = const.tile([P, ROWS * PACK], BF16, align_bytes=64)
+        x_codes = const.tile([P, ROWS], U32, align_bytes=64)
+        x_scales = const.tile([P, ROWS], U8, align_bytes=64)
         w1_grp = const.tile([P, 2, WIDTH, PACK], BF16, align_bytes=64)
         w1_codes = const.tile([P, 2, WIDTH], U32, align_bytes=64)
         w1_scales = const.tile([P, 2, WIDTH], U8, align_bytes=64)
@@ -109,15 +108,15 @@ def tile_causalexpert_pa_kernel(tc, x_attn, cw1, cb1, cw2, cb2, cln_g, cln_b, ou
         w2_scales = const.tile([P, WIDTH], U8, align_bytes=64)
 
         def turn_x(g):
-            xt = accbanks.tile([P, 2, 2, P], F32, tag="acc")
-            for n in range(2):
-                words = x_sb[:, 2 * g + n, :].bitcast(F32)
+            xt = accbanks.tile([P, ROW_TILES, 2, P], F32, tag="acc")
+            for n in range(ROW_TILES):
+                words = x_sb[:, ROW_TILES * g + n, :].bitcast(F32)
                 for u in range(2):
                     nc.tensor.transpose(xt[:, n, u, :], words[:, P * u : P * (u + 1)], ident[:])
             nc.scalar.copy(
                 out=x_grp[:, GROUP_ROWS * PACK * g : GROUP_ROWS * PACK * (g + 1)]
                 .bitcast(F32)
-                .rearrange("p (n r u) -> p n r u", n=2, u=2),
+                .rearrange("p (n r u) -> p n r u", n=ROW_TILES, u=2),
                 in_=xt[:].rearrange("p n u r -> p n r u"),
             )
 
@@ -174,11 +173,11 @@ def tile_causalexpert_pa_kernel(tc, x_attn, cw1, cb1, cw2, cb2, cln_g, cln_b, ou
             out=shift[:], in0=b_raw[:], scalar1=share[:, 0:1], scalar2=0.0, op0=ALU.mult, op1=ALU.add
         )
 
-        cause = const.tile([P, BATCH * LENGTH, PACK], F32)
-        effect = const.tile([P, BATCH * LENGTH, PACK], F32)
+        cause = const.tile([P, ROWS, PACK], F32)
+        effect = const.tile([P, ROWS, PACK], F32)
 
         def project(g):
-            for n in range(2):
+            for n in range(ROW_TILES):
                 for half in range(2):
                     rows = slice(GROUP_ROWS * g + P * n, GROUP_ROWS * g + P * (n + 1))
                     bank = accbanks.tile([P, PACK, P], F32, tag="acc")
@@ -218,7 +217,7 @@ def tile_causalexpert_pa_kernel(tc, x_attn, cw1, cb1, cw2, cb2, cln_g, cln_b, ou
             pre = stream.tile([P, STEP, P * PACK], F32)
             pre_of[s] = pre
             for k in range(STEP):
-                g, span, half, eff, first, last = tiles[STEP * s + k]
+                g, span, half, eff = tiles[STEP * s + k]
                 group_rows = slice(GROUP_ROWS * g, GROUP_ROWS * (g + 1))
                 a_blocks = cause[:, group_rows, :].rearrange("p (n h l) t -> p n h l t", h=2, l=span)
                 e_blocks = effect[:, group_rows, :].rearrange("p (n h l) t -> p n h l t", h=2, l=span)
@@ -295,7 +294,9 @@ def tile_causalexpert_pa_kernel(tc, x_attn, cw1, cb1, cw2, cb2, cln_g, cln_b, ou
 
         def sum_up(s):
             for index in range(STEP * s, STEP * (s + 1)):
-                g, span, half, eff, first, last = tiles[index]
+                g, span, half, eff = tiles[index]
+                first = index == tiles_per_group * g
+                last = index == tiles_per_group * (g + 1) - 1
                 if first:
                     acc_lo = accbanks.tile([P, 2, GROUP_ROWS], F32, tag="acc")
                     acc_hi = accbanks.tile([P, 2, GROUP_ROWS], F32, tag="acc")
@@ -330,7 +331,7 @@ def tile_causalexpert_pa_kernel(tc, x_attn, cw1, cb1, cw2, cb2, cln_g, cln_b, ou
             g = group_ending_in(s)
             if g is None:
                 return
-            for n in range(GROUP_ROWS // P):
+            for n in range(ROW_TILES):
                 back = accbanks.tile([P, WIDTH], F32, tag="acc")
                 back_of[(g, n)] = back
                 for c in range(CHUNKS):
@@ -342,9 +343,9 @@ def tile_causalexpert_pa_kernel(tc, x_attn, cw1, cb1, cw2, cb2, cln_g, cln_b, ou
             g = group_ending_in(s)
             if g is None:
                 return
-            for n in range(GROUP_ROWS // P):
-                raw = stream.tile([P, WIDTH], F32, bufs=2)
-                raw_total = stream.tile([P, 1], F32, bufs=2)
+            for n in range(ROW_TILES):
+                raw = stream.tile([P, WIDTH], F32, bufs=ROW_TILES)
+                raw_total = stream.tile([P, 1], F32, bufs=ROW_TILES)
                 raw_of[(g, n)] = (raw, raw_total)
                 nc.scalar.activation(out=raw[:], in_=back_of[(g, n)][:], func=ACT.Copy, accum_out=raw_total[:])
 
@@ -352,11 +353,11 @@ def tile_causalexpert_pa_kernel(tc, x_attn, cw1, cb1, cw2, cb2, cln_g, cln_b, ou
             g = group_ending_in(s)
             if g is None:
                 return
-            for n in range(GROUP_ROWS // P):
+            for n in range(ROW_TILES):
                 raw, raw_total = raw_of[(g, n)]
-                neg_mean = stream.tile([P, 1], F32, bufs=2)
+                neg_mean = stream.tile([P, 1], F32, bufs=ROW_TILES)
                 nc.vector.tensor_scalar_mul(out=neg_mean[:], in0=raw_total[:], scalar1=-1.0 / WIDTH)
-                result = stream.tile([P, WIDTH], F32, bufs=2)
+                result = stream.tile([P, WIDTH], F32, bufs=ROW_TILES)
                 nc.vector.scalar_tensor_tensor(
                     out=result[:], in0=raw[:], scalar=neg_mean[:, 0:1], in1=gain[:], op0=ALU.add, op1=ALU.mult
                 )
@@ -367,7 +368,8 @@ def tile_causalexpert_pa_kernel(tc, x_attn, cw1, cb1, cw2, cb2, cln_g, cln_b, ou
         def in_range(s):
             return 0 <= s < n_steps
 
-        for now in range(n_steps + 11):
+        last_stage = 10
+        for now in range(n_steps + last_stage + 1):
             if in_range(now - 6):
                 sum_up(now - 6)
             if in_range(now - 2):

from contextlib import ExitStack

import concourse.mybir as mybir
from concourse.masks import make_identity

F32 = mybir.dt.float32
BF16 = mybir.dt.bfloat16
I32 = mybir.dt.int32
U32 = mybir.dt.uint32
U8 = mybir.dt.uint8
FP8X4 = mybir.dt.float8_e4m3fn_x4
ALU = mybir.AluOpType
ACT = mybir.ActivationFunctionType

P = 128
PACK = 4
BATCH, LENGTH, WIDTH = 32, 32, 512
ROWS = BATCH * LENGTH
EPS = 1e-5
CHUNKS = WIDTH // P
GROUP_BATCH = 8
GROUPS = BATCH // GROUP_BATCH
GROUP_ROWS = GROUP_BATCH * LENGTH
ROW_TILES = GROUP_ROWS // P
DIAGONAL = -1
STEP = 4
GPSIMD_ADDS = 1
SCALAR_SCALES = 1

FLOPS = 2 * ROWS * WIDTH * 2 * WIDTH + 2 * BATCH * (LENGTH * (LENGTH + 1) // 2) * WIDTH * WIDTH


def causal_runs():
    runs = [(16, 1, list(range(16)) + [DIAGONAL]), (16, 0, [DIAGONAL])]
    for span in (8, 4, 2, 1):
        runs.append((span, 1, list(range(span))))
    return runs


def tile_causalexpert_pa_kernel(tc, x_attn, cw1, cb1, cw2, cb2, cln_g, cln_b, out):
    nc = tc.nc
    x_rows = x_attn.flatten_outer_dims()
    out_rows = out.flatten_outer_dims()

    tiles = []
    for g in range(GROUPS):
        for span, half, effects in causal_runs():
            for eff in effects:
                tiles.append((g, span, half, eff))
    n_tiles = len(tiles)
    tiles_per_group = n_tiles // GROUPS
    n_steps = n_tiles // STEP
    assert n_steps * STEP == n_tiles

    with ExitStack() as ctx:
        const = ctx.enter_context(tc.tile_pool(name="const", bufs=1))
        stream = ctx.enter_context(tc.tile_pool(name="stream", bufs=3))
        ypool = ctx.enter_context(tc.tile_pool(name="ypool", bufs=4 * STEP))
        zbanks = ctx.enter_context(tc.psum_pool(name="zbanks", bufs=STEP))
        accbanks = ctx.enter_context(tc.psum_pool(name="accbanks", bufs=4))
        ctx.enter_context(tc.manual_schedule())

        x_sb = const.tile([P, ROW_TILES * GROUPS, WIDTH], BF16)
        w1_raw = const.tile([P, 2, PACK, WIDTH], BF16)
        w2_raw = const.tile([P, PACK, WIDTH], BF16)
        cb1_raw = const.tile([P, PACK], BF16)
        cb2_raw = const.tile([P, WIDTH], BF16)
        g_raw = const.tile([P, WIDTH], BF16)
        b_raw = const.tile([P, WIDTH], BF16)

        def load_x(g):
            nc.sync.dma_start(
                out=x_sb[:, ROW_TILES * g : ROW_TILES * (g + 1), :],
                in_=x_rows[GROUP_ROWS * g : GROUP_ROWS * (g + 1), :].rearrange("(n p) k -> p n k", p=P),
            )

        load_x(0)
        for half in range(2):
            for u in range(2):
                first_row = WIDTH * half + 2 * P * u
                nc.sync.dma_start(
                    out=w1_raw[:, half, 2 * u : 2 * u + 2, :],
                    in_=cw1[first_row : first_row + 2 * P, :].rearrange("(q e) c -> q e c", e=2),
                )
        for g in range(1, GROUPS):
            load_x(g)
        nc.sync.dma_start(out=cb1_raw[:], in_=cb1.rearrange("(p t) -> p t", t=PACK))
        nc.sync.dma_start(out=w2_raw[:], in_=cw2.rearrange("(p t) d -> p t d", t=PACK))
        nc.sync.dma_start(out=cb2_raw[:], in_=cb2.partition_broadcast(P))
        nc.sync.dma_start(out=g_raw[:], in_=cln_g.partition_broadcast(P))
        nc.sync.dma_start(out=b_raw[:], in_=cln_b.partition_broadcast(P))

        ident = const.tile([P, P], F32)
        make_identity(nc, ident[:])
        neg_half = const.tile([P, STEP], F32)
        nc.gpsimd.memset(neg_half[:], -0.5)
        lane = const.tile([P, 1], I32)
        nc.gpsimd.iota(lane[:], pattern=[[0, 1]], base=0, channel_multiplier=1)

        x_grp = const.tile([P, ROWS * PACK], BF16, align_bytes=64)
        x_codes = const.tile([P, ROWS], U32, align_bytes=64)
        x_scales = const.tile([P, ROWS], U8, align_bytes=64)
        w1_grp = const.tile([P, 2, WIDTH, PACK], BF16, align_bytes=64)
        w1_codes = const.tile([P, 2, WIDTH], U32, align_bytes=64)
        w1_scales = const.tile([P, 2, WIDTH], U8, align_bytes=64)
        w2_grp = const.tile([P, WIDTH, PACK], BF16, align_bytes=64)
        w2_codes = const.tile([P, WIDTH], U32, align_bytes=64)
        w2_scales = const.tile([P, WIDTH], U8, align_bytes=64)

        def turn_x(g):
            xt = accbanks.tile([P, ROW_TILES, 2, P], F32, tag="acc")
            for n in range(ROW_TILES):
                words = x_sb[:, ROW_TILES * g + n, :].bitcast(F32)
                for u in range(2):
                    nc.tensor.transpose(xt[:, n, u, :], words[:, P * u : P * (u + 1)], ident[:])
            nc.scalar.copy(
                out=x_grp[:, GROUP_ROWS * PACK * g : GROUP_ROWS * PACK * (g + 1)]
                .bitcast(F32)
                .rearrange("p (n r u) -> p n r u", n=ROW_TILES, u=2),
                in_=xt[:].rearrange("p n u r -> p n r u"),
            )

        def quantise_x(g):
            group_rows = slice(GROUP_ROWS * g, GROUP_ROWS * (g + 1))
            nc.vector.quantize_mx(
                out=x_codes[:, group_rows].bitcast(FP8X4),
                scales=x_scales[:, group_rows],
                in_=x_grp[:, GROUP_ROWS * PACK * g : GROUP_ROWS * PACK * (g + 1)],
            )

        def regroup_w1(half, engine_copy):
            engine_copy(
                out=w1_grp[:, half].rearrange("q (t p) k -> q t p k", t=PACK),
                in_=w1_raw[:, half].rearrange("q k (p t) -> q t p k", t=PACK),
            )

        def quantise_w1(half):
            nc.vector.quantize_mx(
                out=w1_codes[:, half].bitcast(FP8X4),
                scales=w1_scales[:, half],
                in_=w1_grp[:, half].rearrange("q c k -> q (c k)"),
            )

        turn_x(0)
        regroup_w1(0, nc.vector.tensor_copy)
        regroup_w1(1, nc.scalar.copy)
        for g in range(1, GROUPS):
            turn_x(g)
        nc.scalar.copy(out=w2_grp[:], in_=w2_raw[:].rearrange("p t d -> p d t"))
        quantise_x(0)
        quantise_w1(0)
        cb1_f = const.tile([P, PACK], F32)
        nc.vector.tensor_copy(out=cb1_f[:], in_=cb1_raw[:])
        position = const.tile([P, 1], I32)
        share = const.tile([P, 1], F32)
        nc.vector.tensor_single_scalar(out=position[:], in_=lane[:], scalar=LENGTH - 1, op=ALU.bitwise_and)
        nc.vector.tensor_copy(out=share[:], in_=position[:])
        nc.vector.tensor_scalar(
            out=share[:], in0=share[:], scalar1=1.0, scalar2=1.0 / LENGTH, op0=ALU.add, op1=ALU.mult
        )
        quantise_w1(1)
        for g in range(1, GROUPS):
            quantise_x(g)

        cb2_f = const.tile([P, WIDTH], F32)
        gain = const.tile([P, WIDTH], F32)
        shift = const.tile([P, WIDTH], F32)
        nc.gpsimd.tensor_scalar(out=cb2_f[:], in0=cb2_raw[:], scalar1=1.0, scalar2=0.0, op0=ALU.mult, op1=ALU.add)
        nc.gpsimd.tensor_scalar(
            out=gain[:], in0=g_raw[:], scalar1=1.0 / LENGTH, scalar2=0.0, op0=ALU.mult, op1=ALU.add
        )
        nc.gpsimd.tensor_scalar(
            out=shift[:], in0=b_raw[:], scalar1=share[:, 0:1], scalar2=0.0, op0=ALU.mult, op1=ALU.add
        )

        cause = const.tile([P, ROWS, PACK], F32)
        effect = const.tile([P, ROWS, PACK], F32)

        def project(g):
            for n in range(ROW_TILES):
                for half in range(2):
                    rows = slice(GROUP_ROWS * g + P * n, GROUP_ROWS * g + P * (n + 1))
                    bank = accbanks.tile([P, PACK, P], F32, tag="acc")
                    for t in range(PACK):
                        cols = slice(P * t, P * (t + 1))
                        nc.tensor.matmul_mx(
                            out=bank[:, t, :],
                            lhsT=w1_codes[:, half, cols].bitcast(FP8X4),
                            lhsT_scale=w1_scales[:, half, cols],
                            rhs=x_codes[:, rows].bitcast(FP8X4),
                            rhs_scale=x_scales[:, rows],
                            start=True,
                            stop=True,
                        )
                    by_row = bank[:].rearrange("p t r -> p r t")
                    if half == 0:
                        nc.vector.tensor_tensor(
                            out=cause[:, rows, :],
                            in0=by_row,
                            in1=cb1_f[:].unsqueeze(1).to_broadcast([P, P, PACK]),
                            op=ALU.add,
                        )
                    else:
                        nc.scalar.copy(out=effect[:, rows, :], in_=by_row)

        project(0)

        total = const.tile([P, n_tiles], F32)
        spread = const.tile([P, n_tiles], F32)
        variance = const.tile([P, n_tiles], F32)
        rstd = const.tile([P, n_tiles], F32)
        pre_of, h2_of, codes_of, scales_of, z_of, y_of, acc_of, summed_of, back_of, raw_of = (
            {}, {}, {}, {}, {}, {}, {}, {}, {}, {},
        )

        def add(s):
            pre = stream.tile([P, STEP, P * PACK], F32)
            pre_of[s] = pre
            for k in range(STEP):
                g, span, half, eff = tiles[STEP * s + k]
                group_rows = slice(GROUP_ROWS * g, GROUP_ROWS * (g + 1))
                a_blocks = cause[:, group_rows, :].rearrange("p (n h l) t -> p n h l t", h=2, l=span)
                e_blocks = effect[:, group_rows, :].rearrange("p (n h l) t -> p n h l t", h=2, l=span)
                if eff == DIAGONAL:
                    e_view = e_blocks[:, :, half, :, :]
                else:
                    e_view = e_blocks[:, :, 0, eff : eff + 1, :].to_broadcast(
                        [P, GROUP_ROWS // (2 * span), span, PACK]
                    )
                adder = nc.gpsimd if k >= STEP - GPSIMD_ADDS else nc.vector
                adder.tensor_tensor(
                    out=pre[:, k, :].rearrange("p (n l t) -> p n l t", l=span, t=PACK),
                    in0=a_blocks[:, :, half, :, :],
                    in1=e_view,
                    op=ALU.add,
                )

        def gelu(s):
            h2 = stream.tile([P, STEP * P * PACK], BF16, align_bytes=64)
            h2_of[s] = h2
            nc.scalar.activation(out=h2[:], in_=pre_of[s][:].rearrange("p k m -> p (k m)"), func=ACT.Gelu)

        def quantise(s):
            h2_codes = stream.tile([P, STEP * P], U32, align_bytes=64)
            h2_scales = stream.tile([P, STEP * P], U8, align_bytes=64)
            codes_of[s], scales_of[s] = h2_codes, h2_scales
            nc.vector.quantize_mx(out=h2_codes[:].bitcast(FP8X4), scales=h2_scales[:], in_=h2_of[s][:])

        def product(s):
            for k in range(STEP):
                z = zbanks.tile([P, WIDTH], F32)
                z_of[STEP * s + k] = z
                pairs = slice(P * k, P * (k + 1))
                nc.tensor.matmul_mx(
                    out=z[:],
                    lhsT=codes_of[s][:, pairs].bitcast(FP8X4),
                    lhsT_scale=scales_of[s][:, pairs],
                    rhs=w2_codes[:].bitcast(FP8X4),
                    rhs_scale=w2_scales[:],
                    start=True,
                    stop=True,
                )

        def bias(s):
            for index in range(STEP * s, STEP * (s + 1)):
                y = ypool.tile([P, WIDTH], F32)
                y_of[index] = y
                nc.vector.scalar_tensor_tensor(
                    out=y[:], in0=z_of[index][:], scalar=1.0, in1=cb2_f[:], op0=ALU.mult, op1=ALU.add,
                    accum_out=total[:, index : index + 1],
                )

        def deviation(s):
            for index in range(STEP * s, STEP * (s + 1)):
                squares = stream.tile([P, WIDTH], BF16)
                nc.scalar.activation(
                    out=squares[:], in_=y_of[index][:], func=ACT.Square, scale=-float(WIDTH),
                    bias=total[:, index : index + 1], accum_out=spread[:, index : index + 1],
                )
            cols = slice(STEP * s, STEP * (s + 1))
            nc.gpsimd.tensor_scalar(
                out=variance[:, cols], in0=spread[:, cols], scalar1=1.0 / WIDTH**3, scalar2=EPS,
                op0=ALU.mult, op1=ALU.add,
            )
            nc.gpsimd.tensor_tensor(out=rstd[:, cols], in0=variance[:, cols], in1=neg_half[:], op=ALU.pow)

        def scale(s):
            for index in range(STEP * s, STEP * (s + 1)):
                y = y_of[index]
                if index % STEP < STEP - SCALAR_SCALES:
                    nc.vector.tensor_scalar_mul(out=y[:], in0=y[:], scalar1=rstd[:, index : index + 1])
                else:
                    nc.scalar.activation(out=y[:], in_=y[:], func=ACT.Copy, scale=rstd[:, index : index + 1])

        def sum_up(s):
            for index in range(STEP * s, STEP * (s + 1)):
                g, span, half, eff = tiles[index]
                first = index == tiles_per_group * g
                last = index == tiles_per_group * (g + 1) - 1
                if first:
                    acc_lo = accbanks.tile([P, 2, GROUP_ROWS], F32, tag="acc")
                    acc_hi = accbanks.tile([P, 2, GROUP_ROWS], F32, tag="acc")
                    acc_of[g] = (acc_lo, acc_hi)
                for c in range(CHUNKS):
                    columns = acc_of[g][c // 2][:, c % 2, :].rearrange("p (n h l) -> p n h l", h=2, l=span)
                    nc.tensor.matmul(
                        out=columns[:, :, half, :],
                        lhsT=y_of[index][:, P * c : P * (c + 1)],
                        rhs=ident[:].rearrange("p (n l) -> p n l", l=span),
                        is_transpose=True,
                        start=(first and c % 2 == 0),
                        stop=(last and c % 2 == 1),
                    )

        def group_ending_in(s):
            for g in range(GROUPS):
                if (tiles_per_group * (g + 1) - 1) // STEP == s:
                    return g
            return None

        def unload(s):
            g = group_ending_in(s)
            if g is None:
                return
            summed = stream.tile([P, CHUNKS, GROUP_ROWS], F32, bufs=2)
            summed_of[g] = summed
            nc.scalar.copy(out=summed[:, 0:2, :], in_=acc_of[g][0][:])
            nc.vector.tensor_copy(out=summed[:, 2:4, :], in_=acc_of[g][1][:])

        def turn_back(s):
            g = group_ending_in(s)
            if g is None:
                return
            for n in range(ROW_TILES):
                back = accbanks.tile([P, WIDTH], F32, tag="acc")
                back_of[(g, n)] = back
                for c in range(CHUNKS):
                    nc.tensor.transpose(
                        back[:, P * c : P * (c + 1)], summed_of[g][:, c, P * n : P * (n + 1)], ident[:]
                    )

        def centre(s):
            g = group_ending_in(s)
            if g is None:
                return
            for n in range(ROW_TILES):
                raw = stream.tile([P, WIDTH], F32, bufs=ROW_TILES)
                raw_total = stream.tile([P, 1], F32, bufs=ROW_TILES)
                raw_of[(g, n)] = (raw, raw_total)
                nc.scalar.activation(out=raw[:], in_=back_of[(g, n)][:], func=ACT.Copy, accum_out=raw_total[:])

        def affine(s):
            g = group_ending_in(s)
            if g is None:
                return
            for n in range(ROW_TILES):
                raw, raw_total = raw_of[(g, n)]
                neg_mean = stream.tile([P, 1], F32, bufs=ROW_TILES)
                nc.vector.tensor_scalar_mul(out=neg_mean[:], in0=raw_total[:], scalar1=-1.0 / WIDTH)
                result = stream.tile([P, WIDTH], F32, bufs=ROW_TILES)
                nc.vector.scalar_tensor_tensor(
                    out=result[:], in0=raw[:], scalar=neg_mean[:, 0:1], in1=gain[:], op0=ALU.add, op1=ALU.mult
                )
                nc.vector.tensor_tensor(out=result[:], in0=result[:], in1=shift[:], op=ALU.add)
                first_row = GROUP_ROWS * g + P * n
                nc.sync.dma_start(out=out_rows[first_row : first_row + P, :], in_=result[:])

        def in_range(s):
            return 0 <= s < n_steps

        last_stage = 10
        for now in range(n_steps + last_stage + 1):
            if in_range(now - 6):
                sum_up(now - 6)
            if in_range(now - 2):
                quantise(now - 2)
                product(now - 2)
            if in_range(now - 3):
                bias(now - 3)
            if in_range(now - 1):
                gelu(now - 1)
            if in_range(now):
                add(now)
            if in_range(now - 4):
                deviation(now - 4)
            if in_range(now - 5):
                scale(now - 5)
            unload(now - 7)
            turn_back(now - 8)
            centre(now - 9)
            affine(now - 10)
            if now == 0:
                nc.vector.quantize_mx(
                    out=w2_codes[:].bitcast(FP8X4), scales=w2_scales[:], in_=w2_grp[:].rearrange("p d t -> p (d t)")
                )
            if now + 1 < GROUPS:
                project(now + 1)
